import numpy as np
import ml_dtypes


def mxq(x, axis, fmt="e4m3"):
    dtype, down = {"e4m3": (ml_dtypes.float8_e4m3fn, 7), "e5m2": (ml_dtypes.float8_e5m2, 14)}[fmt]
    v = np.moveaxis(np.asarray(x, np.float32).astype(ml_dtypes.bfloat16).astype(np.float64), axis, -1)
    blocks = v.reshape(v.shape[:-1] + (-1, 32))
    amax = np.abs(blocks).max(-1, keepdims=True)
    byte = np.maximum(np.where(amax > 0, np.frexp(amax)[1] - 1 + 127, 0) - down, 1)
    scale = np.exp2(byte - 127.0)
    codes = (blocks / scale).astype(np.float32).astype(dtype).astype(np.float64)
    return np.moveaxis((codes * scale).reshape(v.shape), -1, axis)


WIDE = False


def mx_kscale(k):
    if not WIDE:
        return np.ones(k)
    levels = np.array([10, -10, 5, -5, 0])
    a = np.random.permutation(np.resize(levels, k // 512 * 4)).reshape(k // 512, 4)
    idx = np.arange(k)
    return np.exp2(a[idx // 512, idx % 128 // 32])


BF16 = ml_dtypes.bfloat16


def bf(x):
    return np.asarray(x, np.float32).astype(BF16)


def f64(x):
    return np.asarray(x).astype(np.float64)


B, C, K, L, R = 4, 64, 1024, 4, 128


def transition():
    g = np.exp(2.5 * np.random.standard_normal((K, K)))
    return g / g.sum(1, keepdims=True)


def setup_inputs():
    s = mx_kscale(K)
    x = np.random.standard_normal((B, C, K, L)) * 2.0 * s[None, None, :, None]
    return {'x': bf(x.reshape(B, C, K * L)),
            'support0': bf(transition() * s[:, None] / s[None, :]),
            'support1': bf(transition() * s[:, None] / s[None, :])}


def two_hops(xq, a):
    aq = mxq(f64(a).T, 0, 'e4m3')
    x1 = xq @ aq
    x2 = mxq(x1, 2, 'e4m3') @ aq
    return x1, x2


def reference(x, support0, support1):
    xr = f64(x).reshape(B, C, K, L).transpose(0, 3, 1, 2).reshape(B * L, C, K)
    xq = mxq(xr, 2, 'e4m3')
    f1, f2 = two_hops(xq, support0)
    g1, g2 = two_hops(xq, support1)
    return f1, f2, g1, g2

@@ -1,0 +1,197 @@
+from contextlib import ExitStack
+
+import concourse.mybir as mybir
+from concourse.masks import make_identity
+
+F32 = mybir.dt.float32
+BF16 = mybir.dt.bfloat16
+U32 = mybir.dt.uint32
+U8 = mybir.dt.uint8
+FP8X4 = mybir.dt.float8_e4m3fn_x4
+
+P = 128
+PACK = 4
+PAIR = 2
+K_PASS = P * PACK
+NODES = 1024
+ROWS = 1024
+STEPS = 4
+CHANNELS = 64
+PASSES = NODES // K_PASS
+WIDE = 512
+HALVES = ROWS // WIDE
+TILES = WIDE // P
+
+FLOPS = 4 * 2 * ROWS * NODES * NODES
+
+
+def tile_adaptivegcn_pb_kernel(tc, x, support0, support1, out_0, out_1, out_2, out_3):
+    nc = tc.nc
+    supports = (support0, support1)
+    first_out = [o.rearrange("n c w -> (n c) w") for o in (out_0, out_2)]
+    second_out = [o.rearrange("n c w -> (n c) w") for o in (out_1, out_3)]
+
+    with ExitStack() as ctx:
+        keep = ctx.enter_context(tc.tile_pool(name="keep", bufs=1))
+        group_pool = ctx.enter_context(tc.tile_pool(name="group", bufs=4))
+        result_pool = ctx.enter_context(tc.tile_pool(name="result", bufs=6))
+        small_banks = ctx.enter_context(tc.psum_pool(name="small_banks", bufs=4))
+        wide_banks = ctx.enter_context(tc.psum_pool(name="wide_banks", bufs=4))
+
+        identity = keep.tile([P, P], F32, name="identity")
+        make_identity(nc, identity[:])
+
+        x_raw = [keep.tile([P, NODES * STEPS], BF16, name="x_raw%d" % r) for r in range(HALVES)]
+        x_steps = [keep.tile([P, STEPS, NODES], BF16, name="x_steps%d" % r) for r in range(HALVES)]
+        a_raw = [keep.tile([P, PACK, PAIR, NODES], BF16, name="a_raw%d" % s) for s in range(2)]
+
+        def mx_operand(name):
+            codes = keep.tile([P, PASSES, 1024], U32, name=name + "_codes", align_bytes=64)
+            scales = keep.tile([P, PASSES, 1024], U8, name=name + "_scales", align_bytes=64)
+            return codes, scales
+
+        x_mx = mx_operand("x")
+        a_mx = [mx_operand("a%d" % s) for s in range(2)]
+        hop_mx = [mx_operand("hop%d" % s) for s in range(2)]
+
+        x_rows = x.rearrange("b c f -> (b c) f")
+
+        def load_x(r):
+            for g in range(PASSES):
+                cols = slice(g * K_PASS * STEPS, (g + 1) * K_PASS * STEPS)
+                nc.sync.dma_start(out=x_raw[r][:, cols], in_=x_rows[r * P : (r + 1) * P, cols])
+
+        def load_support(s):
+            blocks = supports[s].rearrange("(j p e) v -> j p (e v)", p=P, e=PAIR)
+            for j in range(PACK):
+                nc.sync.dma_start(
+                    out=a_raw[s][:, j, :, :].rearrange("p e v -> p (e v)"), in_=blocks[j]
+                )
+
+        load_x(0)
+        load_support(0)
+        load_x(1)
+        load_support(1)
+
+        def quantise(grouped, operand, g, cols):
+            codes, scales = operand
+            nc.vector.quantize_mx(
+                out=codes[:, g, cols].bitcast(FP8X4),
+                scales=scales[:, g, cols],
+                in_=grouped[:].rearrange("p c t -> p (c t)"),
+            )
+
+        def transpose_words(first, second, g):
+            bank = small_banks.tile([P, 2, PAIR, P], F32, tag="bank")
+            for a, view in enumerate((first, second)):
+                words = view.bitcast(F32)
+                for u in range(PAIR):
+                    start = (PAIR * g + u) * P
+                    nc.tensor.transpose(bank[:, a, u, :], words[:, start : start + P], identity[:])
+            return bank
+
+        def prepare_x(r):
+            for g in range(PASSES):
+                nodes = slice(g * K_PASS, (g + 1) * K_PASS)
+                nc.vector.tensor_copy(
+                    out=x_steps[r][:, :, nodes],
+                    in_=x_raw[r][:].rearrange("p (k l) -> p l k", l=STEPS)[:, :, nodes],
+                )
+            for g in range(PASSES):
+                grouped = group_pool.tile([P, WIDE, PACK], BF16, tag="grouped", align_bytes=64)
+                grouped_words = grouped[:].bitcast(F32)
+                for h in range(STEPS // 2):
+                    bank = transpose_words(x_steps[r][:, 2 * h, :], x_steps[r][:, 2 * h + 1, :], g)
+                    for b in range(2):
+                        first = (b * STEPS + 2 * h) * CHANNELS
+                        nc.scalar.copy(
+                            out=grouped_words[:, first : first + P, :].rearrange(
+                                "p (a c) u -> p a c u", a=2
+                            ),
+                            in_=bank[:, :, :, b * CHANNELS : (b + 1) * CHANNELS].rearrange(
+                                "p a u c -> p a c u"
+                            ),
+                        )
+                quantise(grouped, x_mx, g, slice(r * WIDE, (r + 1) * WIDE))
+
+        def prepare_support(s):
+            for half in range(HALVES):
+                for g in range(PASSES):
+                    grouped = group_pool.tile([P, WIDE, PACK], BF16, tag="grouped", align_bytes=64)
+                    grouped_words = grouped[:].bitcast(F32)
+                    for jj in range(2):
+                        j = 2 * half + jj
+                        bank = transpose_words(a_raw[s][:, j, 0, :], a_raw[s][:, j, 1, :], g)
+                        nc.scalar.copy(
+                            out=grouped_words[:, jj * 2 * P : (jj + 1) * 2 * P, :].rearrange(
+                                "p (a c) u -> p a c u", a=2
+                            ),
+                            in_=bank[:].rearrange("p a u c -> p a c u"),
+                        )
+                    quantise(grouped, a_mx[s], g, slice(half * WIDE, (half + 1) * WIDE))
+
+        def copy_out(turn, out, in_):
+            if turn % 2 == 0:
+                nc.vector.tensor_copy(out=out, in_=in_)
+            else:
+                nc.scalar.copy(out=out, in_=in_)
+
+        def multiply(out, stationary, s_cols, moving, m_cols):
+            for g in range(PASSES):
+                nc.tensor.matmul_mx(
+                    out=out,
+                    lhsT=stationary[0][:, g, s_cols].bitcast(FP8X4),
+                    lhsT_scale=stationary[1][:, g, s_cols],
+                    rhs=moving[0][:, g, m_cols].bitcast(FP8X4),
+                    rhs_scale=moving[1][:, g, m_cols],
+                    start=(g == 0),
+                    stop=(g == PASSES - 1),
+                )
+
+        def first_hop_for_second(s, half):
+            for g in range(PASSES):
+                grouped = group_pool.tile([P, WIDE, PACK], BF16, tag="grouped", align_bytes=64)
+                for i in range(TILES):
+                    rows = slice(half * WIDE + i * P, half * WIDE + (i + 1) * P)
+                    bank = small_banks.tile([P, PACK, P], F32, tag="bank")
+                    for t in range(PACK):
+                        nodes = slice(g * K_PASS + t * P, g * K_PASS + (t + 1) * P)
+                        multiply(bank[:, t, :], a_mx[s], nodes, x_mx, rows)
+                    copy_out(
+                        i,
+                        grouped[:, i * P : (i + 1) * P, :],
+                        bank[:].rearrange("p t m -> p m t"),
+                    )
+                quantise(grouped, hop_mx[s], g, slice(half * WIDE, (half + 1) * WIDE))
+
+        def hop_to_output(operand, s, half, out):
+            for i in range(TILES):
+                rows = slice(half * WIDE + i * P, half * WIDE + (i + 1) * P)
+                result = result_pool.tile([P, NODES], F32, tag="result")
+                for g in range(HALVES):
+                    cols = slice(g * WIDE, (g + 1) * WIDE)
+                    bank = wide_banks.tile([P, WIDE], F32, tag="wide")
+                    multiply(bank[:], operand, rows, a_mx[s], cols)
+                    copy_out(
+                        g,
+                        result[:, cols].rearrange("m (u p e) -> m u p e", u=PAIR, e=PAIR),
+                        bank[:].rearrange("m (u e p) -> m u p e", u=PAIR, e=PAIR),
+                    )
+                nc.sync.dma_start(out=out[rows, :], in_=result[:])
+
+        prepare_x(0)
+        prepare_support(0)
+        first_hop_for_second(0, 0)
+        prepare_x(1)
+        hop_to_output(x_mx, 0, 0, first_out[0])
+        first_hop_for_second(0, 1)
+        prepare_support(1)
+        hop_to_output(x_mx, 0, 1, first_out[0])
+        hop_to_output(hop_mx[0], 0, 0, second_out[0])
+        first_hop_for_second(1, 0)
+        hop_to_output(hop_mx[0], 0, 1, second_out[0])
+        hop_to_output(x_mx, 1, 0, first_out[1])
+        first_hop_for_second(1, 1)
+        hop_to_output(x_mx, 1, 1, first_out[1])
+        hop_to_output(hop_mx[1], 1, 0, second_out[1])
+        hop_to_output(hop_mx[1], 1, 1, second_out[1])

@@ -35,6 +35,7 @@ def tile_adaptivegcn_pb_kernel(tc, x, support0, support1, out_0, out_1, out_2, o
         keep = ctx.enter_context(tc.tile_pool(name="keep", bufs=1))
         group_pool = ctx.enter_context(tc.tile_pool(name="group", bufs=4))
         result_pool = ctx.enter_context(tc.tile_pool(name="result", bufs=6))
+        ordered_pool = ctx.enter_context(tc.tile_pool(name="ordered", bufs=2 * TILES))
         small_banks = ctx.enter_context(tc.psum_pool(name="small_banks", bufs=4))
         wide_banks = ctx.enter_context(tc.psum_pool(name="wide_banks", bufs=4))
 
@@ -148,15 +149,43 @@ def tile_adaptivegcn_pb_kernel(tc, x, support0, support1, out_0, out_1, out_2, o
                     stop=(g == PASSES - 1),
                 )
 
-        def first_hop_for_second(s, half):
+        def row_tile(half, i):
+            return slice(half * WIDE + i * P, half * WIDE + (i + 1) * P)
+
+        def first_hop(s, half):
+            ordered = [
+                ordered_pool.tile([P, NODES], F32, tag="ordered", name="ordered%d" % i)
+                for i in range(TILES)
+            ]
+            for g in range(HALVES):
+                cols = slice(g * WIDE, (g + 1) * WIDE)
+                for i in range(TILES):
+                    bank = wide_banks.tile([P, WIDE], F32, tag="wide")
+                    multiply(bank[:], x_mx, row_tile(half, i), a_mx[s], cols)
+                    copy_out(i, ordered[i][:, cols], bank[:])
+            for i in range(TILES):
+                result = result_pool.tile([P, NODES], F32, tag="result")
+                nc.gpsimd.tensor_scalar(
+                    out=result[:].rearrange("m (j p e) -> m j p e", p=P, e=PAIR),
+                    in0=ordered[i][:].rearrange("m (j e p) -> m j p e", p=P, e=PAIR),
+                    scalar1=1.0,
+                    scalar2=0.0,
+                    op0=mybir.AluOpType.mult,
+                    op1=mybir.AluOpType.add,
+                )
+                nc.sync.dma_start(out=first_out[s][row_tile(half, i), :], in_=result[:])
+            return ordered
+
+        def quantise_first_hop(s, half, ordered):
             for g in range(PASSES):
                 grouped = group_pool.tile([P, WIDE, PACK], BF16, tag="grouped", align_bytes=64)
                 for i in range(TILES):
-                    rows = slice(half * WIDE + i * P, half * WIDE + (i + 1) * P)
                     bank = small_banks.tile([P, PACK, P], F32, tag="bank")
                     for t in range(PACK):
-                        nodes = slice(g * K_PASS + t * P, g * K_PASS + (t + 1) * P)
-                        multiply(bank[:, t, :], a_mx[s], nodes, x_mx, rows)
+                        start = g * K_PASS + t * P
+                        nc.tensor.transpose(
+                            bank[:, t, :], ordered[i][:, start : start + P], identity[:]
+                        )
                     copy_out(
                         i,
                         grouped[:, i * P : (i + 1) * P, :],
@@ -164,34 +193,36 @@ def tile_adaptivegcn_pb_kernel(tc, x, support0, support1, out_0, out_1, out_2, o
                     )
                 quantise(grouped, hop_mx[s], g, slice(half * WIDE, (half + 1) * WIDE))
 
-        def hop_to_output(operand, s, half, out):
+        def second_hop(s, half):
             for i in range(TILES):
-                rows = slice(half * WIDE + i * P, half * WIDE + (i + 1) * P)
                 result = result_pool.tile([P, NODES], F32, tag="result")
                 for g in range(HALVES):
                     cols = slice(g * WIDE, (g + 1) * WIDE)
                     bank = wide_banks.tile([P, WIDE], F32, tag="wide")
-                    multiply(bank[:], operand, rows, a_mx[s], cols)
+                    multiply(bank[:], hop_mx[s], row_tile(half, i), a_mx[s], cols)
                     copy_out(
                         g,
                         result[:, cols].rearrange("m (u p e) -> m u p e", u=PAIR, e=PAIR),
                         bank[:].rearrange("m (u e p) -> m u p e", u=PAIR, e=PAIR),
                     )
-                nc.sync.dma_start(out=out[rows, :], in_=result[:])
+                nc.sync.dma_start(out=second_out[s][row_tile(half, i), :], in_=result[:])
 
         prepare_x(0)
         prepare_support(0)
-        first_hop_for_second(0, 0)
+        hop_00 = first_hop(0, 0)
+
         prepare_x(1)
-        hop_to_output(x_mx, 0, 0, first_out[0])
-        first_hop_for_second(0, 1)
+        quantise_first_hop(0, 0, hop_00)
+        hop_01 = first_hop(0, 1)
+
         prepare_support(1)
-        hop_to_output(x_mx, 0, 1, first_out[0])
-        hop_to_output(hop_mx[0], 0, 0, second_out[0])
-        first_hop_for_second(1, 0)
-        hop_to_output(hop_mx[0], 0, 1, second_out[0])
-        hop_to_output(x_mx, 1, 0, first_out[1])
-        first_hop_for_second(1, 1)
-        hop_to_output(x_mx, 1, 1, first_out[1])
-        hop_to_output(hop_mx[1], 1, 0, second_out[1])
-        hop_to_output(hop_mx[1], 1, 1, second_out[1])
+        quantise_first_hop(0, 1, hop_01)
+        second_hop(0, 0)
+        hop_10 = first_hop(1, 0)
+        hop_11 = first_hop(1, 1)
+
+        quantise_first_hop(1, 0, hop_10)
+        quantise_first_hop(1, 1, hop_11)
+        second_hop(0, 1)
+        second_hop(1, 0)
+        second_hop(1, 1)

@@ -38,6 +38,7 @@ def tile_adaptivegcn_pb_kernel(tc, x, support0, support1, out_0, out_1, out_2, o
         ordered_pool = ctx.enter_context(tc.tile_pool(name="ordered", bufs=2 * TILES))
         small_banks = ctx.enter_context(tc.psum_pool(name="small_banks", bufs=4))
         wide_banks = ctx.enter_context(tc.psum_pool(name="wide_banks", bufs=4))
+        ctx.enter_context(tc.manual_schedule())
 
         identity = keep.tile([P, P], F32, name="identity")
         make_identity(nc, identity[:])
@@ -91,16 +92,40 @@ def tile_adaptivegcn_pb_kernel(tc, x, support0, support1, out_0, out_1, out_2, o
                     nc.tensor.transpose(bank[:, a, u, :], words[:, start : start + P], identity[:])
             return bank
 
-        def prepare_x(r):
+        def gpsimd_copy(out, in_):
+            nc.gpsimd.tensor_scalar(
+                out=out,
+                in0=in_,
+                scalar1=1.0,
+                scalar2=0.0,
+                op0=mybir.AluOpType.mult,
+                op1=mybir.AluOpType.add,
+            )
+
+        def split_time_steps(r, copy):
             for g in range(PASSES):
                 nodes = slice(g * K_PASS, (g + 1) * K_PASS)
-                nc.vector.tensor_copy(
+                copy(
                     out=x_steps[r][:, :, nodes],
                     in_=x_raw[r][:].rearrange("p (k l) -> p l k", l=STEPS)[:, :, nodes],
                 )
+
+        def new_grouped():
+            return [
+                group_pool.tile(
+                    [P, WIDE, PACK], BF16, tag="grouped", name="grouped%d" % g, align_bytes=64
+                )
+                for g in range(PASSES)
+            ]
+
+        def quantise_both(grouped, operand, cols):
             for g in range(PASSES):
-                grouped = group_pool.tile([P, WIDE, PACK], BF16, tag="grouped", align_bytes=64)
-                grouped_words = grouped[:].bitcast(F32)
+                quantise(grouped[g], operand, g, cols)
+
+        def prepare_x(r):
+            grouped = new_grouped()
+            for g in range(PASSES):
+                grouped_words = grouped[g][:].bitcast(F32)
                 for h in range(STEPS // 2):
                     bank = transpose_words(x_steps[r][:, 2 * h, :], x_steps[r][:, 2 * h + 1, :], g)
                     for b in range(2):
@@ -113,13 +138,13 @@ def tile_adaptivegcn_pb_kernel(tc, x, support0, support1, out_0, out_1, out_2, o
                                 "p a u c -> p a c u"
                             ),
                         )
-                quantise(grouped, x_mx, g, slice(r * WIDE, (r + 1) * WIDE))
+            quantise_both(grouped, x_mx, slice(r * WIDE, (r + 1) * WIDE))
 
         def prepare_support(s):
             for half in range(HALVES):
+                grouped = new_grouped()
                 for g in range(PASSES):
-                    grouped = group_pool.tile([P, WIDE, PACK], BF16, tag="grouped", align_bytes=64)
-                    grouped_words = grouped[:].bitcast(F32)
+                    grouped_words = grouped[g][:].bitcast(F32)
                     for jj in range(2):
                         j = 2 * half + jj
                         bank = transpose_words(a_raw[s][:, j, 0, :], a_raw[s][:, j, 1, :], g)
@@ -129,7 +154,7 @@ def tile_adaptivegcn_pb_kernel(tc, x, support0, support1, out_0, out_1, out_2, o
                             ),
                             in_=bank[:].rearrange("p a u c -> p a c u"),
                         )
-                    quantise(grouped, a_mx[s], g, slice(half * WIDE, (half + 1) * WIDE))
+                quantise_both(grouped, a_mx[s], slice(half * WIDE, (half + 1) * WIDE))
 
         def copy_out(turn, out, in_):
             if turn % 2 == 0:
@@ -165,20 +190,16 @@ def tile_adaptivegcn_pb_kernel(tc, x, support0, support1, out_0, out_1, out_2, o
                     copy_out(i, ordered[i][:, cols], bank[:])
             for i in range(TILES):
                 result = result_pool.tile([P, NODES], F32, tag="result")
-                nc.gpsimd.tensor_scalar(
+                gpsimd_copy(
                     out=result[:].rearrange("m (j p e) -> m j p e", p=P, e=PAIR),
-                    in0=ordered[i][:].rearrange("m (j e p) -> m j p e", p=P, e=PAIR),
-                    scalar1=1.0,
-                    scalar2=0.0,
-                    op0=mybir.AluOpType.mult,
-                    op1=mybir.AluOpType.add,
+                    in_=ordered[i][:].rearrange("m (j e p) -> m j p e", p=P, e=PAIR),
                 )
                 nc.sync.dma_start(out=first_out[s][row_tile(half, i), :], in_=result[:])
             return ordered
 
         def quantise_first_hop(s, half, ordered):
+            grouped = new_grouped()
             for g in range(PASSES):
-                grouped = group_pool.tile([P, WIDE, PACK], BF16, tag="grouped", align_bytes=64)
                 for i in range(TILES):
                     bank = small_banks.tile([P, PACK, P], F32, tag="bank")
                     for t in range(PACK):
@@ -188,10 +209,10 @@ def tile_adaptivegcn_pb_kernel(tc, x, support0, support1, out_0, out_1, out_2, o
                         )
                     copy_out(
                         i,
-                        grouped[:, i * P : (i + 1) * P, :],
+                        grouped[g][:, i * P : (i + 1) * P, :],
                         bank[:].rearrange("p t m -> p m t"),
                     )
-                quantise(grouped, hop_mx[s], g, slice(half * WIDE, (half + 1) * WIDE))
+            quantise_both(grouped, hop_mx[s], slice(half * WIDE, (half + 1) * WIDE))
 
         def second_hop(s, half):
             for i in range(TILES):
@@ -207,22 +228,24 @@ def tile_adaptivegcn_pb_kernel(tc, x, support0, support1, out_0, out_1, out_2, o
                     )
                 nc.sync.dma_start(out=second_out[s][row_tile(half, i), :], in_=result[:])
 
+        split_time_steps(0, nc.vector.tensor_copy)
         prepare_x(0)
         prepare_support(0)
+        split_time_steps(1, gpsimd_copy)
         hop_00 = first_hop(0, 0)
 
-        prepare_x(1)
-        quantise_first_hop(0, 0, hop_00)
-        hop_01 = first_hop(0, 1)
-
         prepare_support(1)
-        quantise_first_hop(0, 1, hop_01)
-        second_hop(0, 0)
+        quantise_first_hop(0, 0, hop_00)
         hop_10 = first_hop(1, 0)
+
+        prepare_x(1)
+        quantise_first_hop(1, 0, hop_10)
+        second_hop(0, 0)
+        hop_01 = first_hop(0, 1)
         hop_11 = first_hop(1, 1)
 
-        quantise_first_hop(1, 0, hop_10)
+        quantise_first_hop(0, 1, hop_01)
         quantise_first_hop(1, 1, hop_11)
-        second_hop(0, 1)
         second_hop(1, 0)
+        second_hop(0, 1)
         second_hop(1, 1)

from contextlib import ExitStack

import concourse.mybir as mybir
from concourse.masks import make_identity

F32 = mybir.dt.float32
BF16 = mybir.dt.bfloat16
U32 = mybir.dt.uint32
U8 = mybir.dt.uint8
FP8X4 = mybir.dt.float8_e4m3fn_x4

P = 128
PACK = 4
PAIR = 2
K_PASS = P * PACK
NODES = 1024
ROWS = 1024
STEPS = 4
CHANNELS = 64
PASSES = NODES // K_PASS
WIDE = 512
HALVES = ROWS // WIDE
TILES = WIDE // P

FLOPS = 4 * 2 * ROWS * NODES * NODES


def tile_adaptivegcn_pb_kernel(tc, x, support0, support1, out_0, out_1, out_2, out_3):
    nc = tc.nc
    supports = (support0, support1)
    first_out = [o.rearrange("n c w -> (n c) w") for o in (out_0, out_2)]
    second_out = [o.rearrange("n c w -> (n c) w") for o in (out_1, out_3)]

    with ExitStack() as ctx:
        keep = ctx.enter_context(tc.tile_pool(name="keep", bufs=1))
        group_pool = ctx.enter_context(tc.tile_pool(name="group", bufs=4))
        result_pool = ctx.enter_context(tc.tile_pool(name="result", bufs=6))
        ordered_pool = ctx.enter_context(tc.tile_pool(name="ordered", bufs=2 * TILES))
        small_banks = ctx.enter_context(tc.psum_pool(name="small_banks", bufs=4))
        wide_banks = ctx.enter_context(tc.psum_pool(name="wide_banks", bufs=4))
        ctx.enter_context(tc.manual_schedule())

        identity = keep.tile([P, P], F32, name="identity")
        make_identity(nc, identity[:])

        x_raw = [keep.tile([P, NODES * STEPS], BF16, name="x_raw%d" % r) for r in range(HALVES)]
        x_steps = [keep.tile([P, STEPS, NODES], BF16, name="x_steps%d" % r) for r in range(HALVES)]
        a_raw = [keep.tile([P, PACK, PAIR, NODES], BF16, name="a_raw%d" % s) for s in range(2)]

        def mx_operand(name):
            codes = keep.tile([P, PASSES, 1024], U32, name=name + "_codes", align_bytes=64)
            scales = keep.tile([P, PASSES, 1024], U8, name=name + "_scales", align_bytes=64)
            return codes, scales

        x_mx = mx_operand("x")
        a_mx = [mx_operand("a%d" % s) for s in range(2)]
        hop_mx = [mx_operand("hop%d" % s) for s in range(2)]

        x_rows = x.rearrange("b c f -> (b c) f")

        def load_x(r):
            for g in range(PASSES):
                cols = slice(g * K_PASS * STEPS, (g + 1) * K_PASS * STEPS)
                nc.sync.dma_start(out=x_raw[r][:, cols], in_=x_rows[r * P : (r + 1) * P, cols])

        def load_support(s):
            blocks = supports[s].rearrange("(j p e) v -> j p (e v)", p=P, e=PAIR)
            for j in range(PACK):
                nc.sync.dma_start(
                    out=a_raw[s][:, j, :, :].rearrange("p e v -> p (e v)"), in_=blocks[j]
                )

        load_x(0)
        load_support(0)
        load_x(1)
        load_support(1)

        def quantise(grouped, operand, g, cols):
            codes, scales = operand
            nc.vector.quantize_mx(
                out=codes[:, g, cols].bitcast(FP8X4),
                scales=scales[:, g, cols],
                in_=grouped[:].rearrange("p c t -> p (c t)"),
            )

        def transpose_words(first, second, g):
            bank = small_banks.tile([P, 2, PAIR, P], F32, tag="bank")
            for a, view in enumerate((first, second)):
                words = view.bitcast(F32)
                for u in range(PAIR):
                    start = (PAIR * g + u) * P
                    nc.tensor.transpose(bank[:, a, u, :], words[:, start : start + P], identity[:])
            return bank

        def gpsimd_copy(out, in_):
            nc.gpsimd.tensor_scalar(
                out=out,
                in0=in_,
                scalar1=1.0,
                scalar2=0.0,
                op0=mybir.AluOpType.mult,
                op1=mybir.AluOpType.add,
            )

        def split_time_steps(r, copy):
            for g in range(PASSES):
                nodes = slice(g * K_PASS, (g + 1) * K_PASS)
                copy(
                    out=x_steps[r][:, :, nodes],
                    in_=x_raw[r][:].rearrange("p (k l) -> p l k", l=STEPS)[:, :, nodes],
                )

        def new_grouped():
            return [
                group_pool.tile(
                    [P, WIDE, PACK], BF16, tag="grouped", name="grouped%d" % g, align_bytes=64
                )
                for g in range(PASSES)
            ]

        def quantise_both(grouped, operand, cols):
            for g in range(PASSES):
                quantise(grouped[g], operand, g, cols)

        def prepare_x(r):
            grouped = new_grouped()
            for g in range(PASSES):
                grouped_words = grouped[g][:].bitcast(F32)
                for h in range(STEPS // 2):
                    bank = transpose_words(x_steps[r][:, 2 * h, :], x_steps[r][:, 2 * h + 1, :], g)
                    for b in range(2):
                        first = (b * STEPS + 2 * h) * CHANNELS
                        nc.scalar.copy(
                            out=grouped_words[:, first : first + P, :].rearrange(
                                "p (a c) u -> p a c u", a=2
                            ),
                            in_=bank[:, :, :, b * CHANNELS : (b + 1) * CHANNELS].rearrange(
                                "p a u c -> p a c u"
                            ),
                        )
            quantise_both(grouped, x_mx, slice(r * WIDE, (r + 1) * WIDE))

        def prepare_support(s):
            for half in range(HALVES):
                grouped = new_grouped()
                for g in range(PASSES):
                    grouped_words = grouped[g][:].bitcast(F32)
                    for jj in range(2):
                        j = 2 * half + jj
                        bank = transpose_words(a_raw[s][:, j, 0, :], a_raw[s][:, j, 1, :], g)
                        nc.scalar.copy(
                            out=grouped_words[:, jj * 2 * P : (jj + 1) * 2 * P, :].rearrange(
                                "p (a c) u -> p a c u", a=2
                            ),
                            in_=bank[:].rearrange("p a u c -> p a c u"),
                        )
                quantise_both(grouped, a_mx[s], slice(half * WIDE, (half + 1) * WIDE))

        def copy_out(turn, out, in_):
            if turn % 2 == 0:
                nc.vector.tensor_copy(out=out, in_=in_)
            else:
                nc.scalar.copy(out=out, in_=in_)

        def multiply(out, stationary, s_cols, moving, m_cols):
            for g in range(PASSES):
                nc.tensor.matmul_mx(
                    out=out,
                    lhsT=stationary[0][:, g, s_cols].bitcast(FP8X4),
                    lhsT_scale=stationary[1][:, g, s_cols],
                    rhs=moving[0][:, g, m_cols].bitcast(FP8X4),
                    rhs_scale=moving[1][:, g, m_cols],
                    start=(g == 0),
                    stop=(g == PASSES - 1),
                )

        def row_tile(half, i):
            return slice(half * WIDE + i * P, half * WIDE + (i + 1) * P)

        def first_hop(s, half):
            ordered = [
                ordered_pool.tile([P, NODES], F32, tag="ordered", name="ordered%d" % i)
                for i in range(TILES)
            ]
            for g in range(HALVES):
                cols = slice(g * WIDE, (g + 1) * WIDE)
                for i in range(TILES):
                    bank = wide_banks.tile([P, WIDE], F32, tag="wide")
                    multiply(bank[:], x_mx, row_tile(half, i), a_mx[s], cols)
                    copy_out(i, ordered[i][:, cols], bank[:])
            for i in range(TILES):
                result = result_pool.tile([P, NODES], F32, tag="result")
                gpsimd_copy(
                    out=result[:].rearrange("m (j p e) -> m j p e", p=P, e=PAIR),
                    in_=ordered[i][:].rearrange("m (j e p) -> m j p e", p=P, e=PAIR),
                )
                nc.sync.dma_start(out=first_out[s][row_tile(half, i), :], in_=result[:])
            return ordered

        def quantise_first_hop(s, half, ordered):
            grouped = new_grouped()
            for g in range(PASSES):
                for i in range(TILES):
                    bank = small_banks.tile([P, PACK, P], F32, tag="bank")
                    for t in range(PACK):
                        start = g * K_PASS + t * P
                        nc.tensor.transpose(
                            bank[:, t, :], ordered[i][:, start : start + P], identity[:]
                        )
                    copy_out(
                        i,
                        grouped[g][:, i * P : (i + 1) * P, :],
                        bank[:].rearrange("p t m -> p m t"),
                    )
            quantise_both(grouped, hop_mx[s], slice(half * WIDE, (half + 1) * WIDE))

        def second_hop(s, half):
            for i in range(TILES):
                result = result_pool.tile([P, NODES], F32, tag="result")
                for g in range(HALVES):
                    cols = slice(g * WIDE, (g + 1) * WIDE)
                    bank = wide_banks.tile([P, WIDE], F32, tag="wide")
                    multiply(bank[:], hop_mx[s], row_tile(half, i), a_mx[s], cols)
                    copy_out(
                        g,
                        result[:, cols].rearrange("m (u p e) -> m u p e", u=PAIR, e=PAIR),
                        bank[:].rearrange("m (u e p) -> m u p e", u=PAIR, e=PAIR),
                    )
                nc.sync.dma_start(out=second_out[s][row_tile(half, i), :], in_=result[:])

        split_time_steps(0, nc.vector.tensor_copy)
        prepare_x(0)
        prepare_support(0)
        split_time_steps(1, gpsimd_copy)
        hop_00 = first_hop(0, 0)

        prepare_support(1)
        quantise_first_hop(0, 0, hop_00)
        hop_10 = first_hop(1, 0)

        prepare_x(1)
        quantise_first_hop(1, 0, hop_10)
        second_hop(0, 0)
        hop_01 = first_hop(0, 1)
        hop_11 = first_hop(1, 1)

        quantise_first_hop(0, 1, hop_01)
        quantise_first_hop(1, 1, hop_11)
        second_hop(1, 0)
        second_hop(0, 1)
        second_hop(1, 1)
